import numpy as np
import ml_dtypes


def mxq(x, axis, fmt="e4m3"):
    dtype, down = {"e4m3": (ml_dtypes.float8_e4m3fn, 7), "e5m2": (ml_dtypes.float8_e5m2, 14)}[fmt]
    v = np.moveaxis(np.asarray(x, np.float32).astype(ml_dtypes.bfloat16).astype(np.float64), axis, -1)
    blocks = v.reshape(v.shape[:-1] + (-1, 32))
    amax = np.abs(blocks).max(-1, keepdims=True)
    byte = np.maximum(np.where(amax > 0, np.frexp(amax)[1] - 1 + 127, 0) - down, 1)
    scale = np.exp2(byte - 127.0)
    codes = (blocks / scale).astype(np.float32).astype(dtype).astype(np.float64)
    return np.moveaxis((codes * scale).reshape(v.shape), -1, axis)


WIDE = False


def mx_kscale(k):
    if not WIDE:
        return np.ones(k)
    levels = np.array([10, -10, 5, -5, 0])
    a = np.random.permutation(np.resize(levels, k // 512 * 4)).reshape(k // 512, 4)
    idx = np.arange(k)
    return np.exp2(a[idx // 512, idx % 128 // 32])


BF16 = ml_dtypes.bfloat16


def bf(x):
    return np.asarray(x, np.float32).astype(BF16)


def f64(x):
    return np.asarray(x).astype(np.float64)


E2M1 = np.array([0.0, 0.5, 1.0, 1.5, 2.0, 3.0, 4.0, 6.0, -0.0, -0.5, -1.0, -1.5, -2.0, -3.0, -4.0, -6.0])


def pack_weight(w, fmt):
    k, n = w.shape
    w = f64(bf(w)).reshape(k // 32, 32, n)
    amax = np.abs(w).max(1)
    if fmt == "e4m3":
        byte = np.frexp(amax)[1] - 1 + 127 - 7
    else:
        mant, ex = np.frexp(amax / 6.0)
        byte = np.where(mant > 0.5, ex, ex - 1) + 127
    byte = np.clip(np.where(amax > 0, byte, 1), 1, 254)
    scaled = (w * np.exp2(127.0 - byte)[:, None, :]).reshape(k, n).astype(np.float32)
    by_word = np.ascontiguousarray(scaled.reshape(k // 512, 128, 4, n).transpose(0, 1, 3, 2))
    if fmt == "e4m3":
        words = by_word.astype(ml_dtypes.float8_e4m3fn).view(np.uint8)
    else:
        c = by_word.astype(ml_dtypes.float4_e2m1fn).view(np.uint8) & 0xF
        words = c[..., 0::2] | (c[..., 1::2] << 4)
    return np.ascontiguousarray(words), np.ascontiguousarray(byte.astype(np.uint8).reshape(k // 512, 16, n))


def unpack_weight(words, scales, fmt):
    g, p, n, _ = words.shape
    if fmt == "e4m3":
        vals = np.ascontiguousarray(words).view(ml_dtypes.float8_e4m3fn).astype(np.float64)
    else:
        nib = np.empty((g, p, n, 4), np.uint8)
        nib[..., 0::2] = words & 0xF
        nib[..., 1::2] = words >> 4
        vals = E2M1[nib]
    vals = vals * np.repeat(np.exp2(scales.astype(np.float64) - 127.0), 8, axis=1)[..., None]
    return vals.transpose(0, 1, 3, 2).reshape(g * 512, n)

def pack4(w):
    words, scales = pack_weight(w, "e2m1")
    return words.reshape(words.shape[0], 128, -1), scales


def unpack4(words, scales):
    return unpack_weight(words.reshape(words.shape[0], 128, -1, 2), scales, "e2m1")


B, D, L0, L1, L2 = 4096, 512, 32, 512, 1024
KC = L1 + D
LN_EPS = 1e-5


def log_softmax(v):
    sh = v - v.max(-1, keepdims=True)
    return sh - np.log(np.exp(sh).sum(-1, keepdims=True))


def setup_inputs():
    s = mx_kscale(D)
    w = np.random.standard_normal((L2, KC)) * 1.5 / np.sqrt(KC)
    w[:, L1:] /= s
    mid_logits = bf(np.random.standard_normal((B, L1)) * 3.0)
    x = bf(np.random.standard_normal((B, D)) * s)
    words, scales = pack4(np.ascontiguousarray(w.T))
    return {"mid_logits": mid_logits, "x": x,
            "W2_words": words, "W2_scales": scales, "b2": bf(np.random.standard_normal(L2) * 0.5)}


def reference(mid_logits, x, W2_words, W2_scales, b2):
    h = np.maximum(f64(mid_logits), 0.0)
    mu = h.mean(-1, keepdims=True)
    var = h.var(-1, keepdims=True)
    hn = (h - mu) / np.sqrt(var + LN_EPS)
    c = np.concatenate([hn, f64(x)], axis=1)
    li = (mxq(c, 1, "e4m3") @ unpack4(W2_words, W2_scales)) + f64(b2)
    return log_softmax(li)

@@ -1,0 +1,206 @@
+from contextlib import ExitStack
+
+import concourse.mybir as mybir
+from concourse.masks import make_identity
+
+F32 = mybir.dt.float32
+BF16 = mybir.dt.bfloat16
+I32 = mybir.dt.int32
+U32 = mybir.dt.uint32
+U8 = mybir.dt.uint8
+FP8X4 = mybir.dt.float8_e4m3fn_x4
+FP4X4 = mybir.dt.float4_e2m1fn_x4
+ACT = mybir.ActivationFunctionType
+ALU = mybir.AluOpType
+
+P = 128
+ROWS = 4096
+D_HALF = 512
+N_OUT = 1024
+BANK = 512
+PASSES = 2
+WORDS = D_HALF // 2
+TILES = ROWS // P
+LOAD_TILES = 4
+STORE_TILES = 2
+LOG_TILES = 8
+LN_EPS = 1e-5
+
+FLOPS = 2 * ROWS * (PASSES * D_HALF) * N_OUT
+
+LAG_SQUARES = 1
+LAG_NORMALISE = 2
+LAG_TRANSPOSE = 3
+LAG_QUANTISE = 4
+LAG_MULTIPLY = 5
+LAG_BIAS_MAX = 6
+LAG_EXP = 7
+LAG_SUBTRACT = LAG_EXP + LOG_TILES
+
+
+def tile_bhcn_awx_pa_t_kernel(tc, mid_logits, x, W2_words, W2_scales, b2, out):
+    nc = tc.nc
+    mid_rows = mid_logits.rearrange("(p t) k -> p t k", t=TILES)
+    x_rows = x.rearrange("(p t) k -> p t k", t=TILES)
+    out_rows = out.rearrange("(p t) n -> p t n", t=TILES)
+
+    with ExitStack() as ctx:
+        ctx.enter_context(tc.manual_schedule())
+        keep = ctx.enter_context(tc.tile_pool(name="keep", bufs=1))
+        work = ctx.enter_context(tc.tile_pool(name="work", bufs=3))
+        logits = ctx.enter_context(tc.tile_pool(name="logits", bufs=7))
+        psum_t = ctx.enter_context(tc.psum_pool(name="psum_t", bufs=2))
+        psum_mm = ctx.enter_context(tc.psum_pool(name="psum_mm", bufs=3))
+
+        act = keep.tile([P, TILES, D_HALF], BF16)
+        x_sb = keep.tile([P, TILES, D_HALF], BF16)
+        w_words = keep.tile([P, PASSES, 2 * N_OUT], U8, align_bytes=64)
+        w_scales = keep.tile([P, PASSES, N_OUT], U8, align_bytes=64)
+        bias = keep.tile([P, N_OUT], BF16)
+        identity = keep.tile([P, P], F32)
+        minus_half = keep.tile([P, 1], F32)
+        row_sum = keep.tile([P, TILES], F32)
+        neg_mean = keep.tile([P, TILES], F32)
+        sq_sum = keep.tile([P, TILES], F32)
+        var_eps = keep.tile([P, TILES], F32)
+        inv_std = keep.tile([P, TILES], F32)
+        neg_max = keep.tile([P, TILES], F32)
+        exp_sum = keep.tile([P, TILES], F32)
+        log_sum = keep.tile([P, TILES], F32)
+        shift = keep.tile([P, TILES], F32)
+
+        nc.vector.memset(w_scales[:].bitcast(I32), 0)
+        nc.vector.memset(minus_half[:], -0.5)
+        make_identity(nc, identity[:])
+
+        def load_rows(first):
+            tiles = slice(first, first + LOAD_TILES)
+            nc.sync.dma_start(out=act[:, tiles, :], in_=mid_rows[:, tiles, :])
+            if first == 0:
+                load_weight()
+            nc.sync.dma_start(out=x_sb[:, tiles, :], in_=x_rows[:, tiles, :])
+
+        def load_weight():
+            scale_words = W2_scales.bitcast(I32)
+            for quadrant in range(4):
+                nc.sync.dma_start(
+                    out=w_scales[32 * quadrant : 32 * quadrant + 4, :, :].bitcast(I32),
+                    in_=scale_words[:, 4 * quadrant : 4 * quadrant + 4, :].rearrange("g q w -> q g w"),
+                )
+            nc.sync.dma_start(out=w_words[:].bitcast(I32), in_=W2_words.bitcast(I32).rearrange("g p w -> p g w"))
+
+        nc.scalar.dma_start(out=bias[:], in_=b2.partition_broadcast(P))
+        for first in range(0, TILES, LOAD_TILES):
+            load_rows(first)
+
+        turned = {}
+        codes = {}
+        sums = {}
+        li_pairs = {}
+
+        def li(t):
+            return li_pairs[t // STORE_TILES][:, t % STORE_TILES, :]
+
+        def col(t):
+            return slice(t, t + 1)
+
+        def relu_sum(t):
+            nc.scalar.activation(out=act[:, t, :], in_=act[:, t, :], func=ACT.Relu, accum_out=row_sum[:, col(t)])
+            nc.gpsimd.tensor_scalar(
+                out=neg_mean[:, col(t)], in0=row_sum[:, col(t)],
+                scalar1=-1.0 / D_HALF, scalar2=0.0, op0=ALU.mult, op1=ALU.add,
+            )
+
+        def squares(t):
+            unread = work.tile([P, D_HALF], BF16, name="unread_sq")
+            nc.scalar.activation(
+                out=unread[:], in_=act[:, t, :], func=ACT.Square, bias=neg_mean[:, col(t)], accum_out=sq_sum[:, col(t)]
+            )
+            nc.gpsimd.tensor_scalar(
+                out=var_eps[:, col(t)], in0=sq_sum[:, col(t)],
+                scalar1=1.0 / D_HALF, scalar2=LN_EPS, op0=ALU.mult, op1=ALU.add,
+            )
+            nc.gpsimd.tensor_tensor(out=inv_std[:, col(t)], in0=var_eps[:, col(t)], in1=minus_half[:], op=ALU.pow)
+
+        def normalise(t):
+            nc.vector.tensor_scalar(
+                out=act[:, t, :], in0=act[:, t, :],
+                scalar1=neg_mean[:, col(t)], scalar2=inv_std[:, col(t)], op0=ALU.add, op1=ALU.mult,
+            )
+
+        def transpose(t):
+            turned[t] = psum_t.tile([P, PASSES, 2, P], F32, name="turned")
+            for g, rows in enumerate((act, x_sb)):
+                words = rows[:, t, :].bitcast(F32)
+                for u in range(2):
+                    nc.tensor.transpose(turned[t][:, g, u, :], words[:, u:WORDS:2], identity[:])
+
+        def quantise(t):
+            grouped = work.tile([P, PASSES * P * 4], BF16, name="grouped", align_bytes=64)
+            nc.scalar.copy(
+                out=grouped[:].bitcast(F32).rearrange("p (g r u) -> p g r u", g=PASSES, u=2),
+                in_=turned[t][:].rearrange("p g u r -> p g r u"),
+            )
+            words = work.tile([P, PASSES * P], U32, name="c_words", align_bytes=64)
+            plane = work.tile([P, PASSES * P], U8, name="c_scales", align_bytes=64)
+            nc.vector.quantize_mx(out=words[:].bitcast(FP8X4), scales=plane[:], in_=grouped[:])
+            codes[t] = (words, plane)
+
+        def multiply(t):
+            words, plane = codes[t]
+            sums[t] = []
+            for half in range(N_OUT // BANK):
+                acc = psum_mm.tile([P, BANK], F32, name="acc%d" % half)
+                for g in range(PASSES):
+                    nc.tensor.matmul_mx(
+                        out=acc[:],
+                        lhsT=words[:, g * P : (g + 1) * P].bitcast(FP8X4),
+                        lhsT_scale=plane[:, g * P : (g + 1) * P],
+                        rhs=w_words[:, g, 2 * BANK * half : 2 * BANK * (half + 1)].bitcast(FP4X4),
+                        rhs_scale=w_scales[:, g, BANK * half : BANK * (half + 1)],
+                        start=(g == 0),
+                        stop=(g == PASSES - 1),
+                    )
+                sums[t].append(acc)
+
+        def bias_max(t):
+            if t % STORE_TILES == 0:
+                li_pairs[t // STORE_TILES] = logits.tile([P, STORE_TILES, N_OUT], F32, name="li_pair")
+            for half, acc in enumerate(sums[t]):
+                cols = slice(BANK * half, BANK * (half + 1))
+                nc.vector.tensor_tensor(out=li(t)[:, cols], in0=acc[:], in1=bias[:, cols], op=ALU.add)
+            nc.vector.tensor_reduce(
+                out=neg_max[:, col(t)], in_=li(t), axis=mybir.AxisListType.X, op=ALU.max, negate=True
+            )
+
+        def exponentials(t):
+            unread = work.tile([P, N_OUT], BF16, name="unread_exp")
+            nc.scalar.activation(
+                out=unread[:], in_=li(t), func=ACT.Exp, bias=neg_max[:, col(t)], accum_out=exp_sum[:, col(t)]
+            )
+            if t % LOG_TILES == LOG_TILES - 1:
+                group = slice(t + 1 - LOG_TILES, t + 1)
+                nc.scalar.activation(out=log_sum[:, group], in_=exp_sum[:, group], func=ACT.Ln)
+
+        def subtract(t):
+            if t % LOG_TILES == 0:
+                group = slice(t, t + LOG_TILES)
+                nc.vector.tensor_tensor(out=shift[:, group], in0=neg_max[:, group], in1=log_sum[:, group], op=ALU.subtract)
+            nc.vector.tensor_scalar_add(out=li(t), in0=li(t), scalar1=shift[:, col(t)])
+            if t % STORE_TILES == STORE_TILES - 1:
+                nc.sync.dma_start(out=out_rows[:, t + 1 - STORE_TILES : t + 1, :], in_=li_pairs[t // STORE_TILES][:])
+
+        def run(stage, t):
+            if 0 <= t < TILES:
+                stage(t)
+
+        for turn in range(TILES + LAG_SUBTRACT):
+            run(exponentials, turn - LAG_EXP)
+            run(bias_max, turn - LAG_BIAS_MAX)
+            run(multiply, turn - LAG_MULTIPLY)
+            run(subtract, turn - LAG_SUBTRACT)
+            run(transpose, turn - LAG_TRANSPOSE)
+            run(normalise, turn - LAG_NORMALISE)
+            run(quantise, turn - LAG_QUANTISE)
+            run(relu_sum, turn)
+            run(squares, turn - LAG_SQUARES)

@@ -1,3 +1,4 @@
+import math
 from contextlib import ExitStack
 
 import concourse.mybir as mybir
@@ -23,7 +24,8 @@ WORDS = D_HALF // 2
 TILES = ROWS // P
 LOAD_TILES = 4
 STORE_TILES = 2
-LOG_TILES = 8
+NEWTON_STEPS = 3
+LOG_TILES = 1 + NEWTON_STEPS
 LN_EPS = 1e-5
 
 FLOPS = 2 * ROWS * (PASSES * D_HALF) * N_OUT
@@ -35,7 +37,11 @@ LAG_QUANTISE = 4
 LAG_MULTIPLY = 5
 LAG_BIAS_MAX = 6
 LAG_EXP = 7
-LAG_SUBTRACT = LAG_EXP + LOG_TILES
+LAG_LOG = LAG_EXP + LOG_TILES - 1
+LAG_SUBTRACT = LAG_LOG + LOG_TILES
+
+GUESS_SCALE = math.log(2.0) / 2.0**23
+GUESS_OFFSET = math.log(2.0) * (0.043 - 127.0)
 
 
 def tile_bhcn_awx_pa_t_kernel(tc, mid_logits, x, W2_words, W2_scales, b2, out):
@@ -67,6 +73,8 @@ def tile_bhcn_awx_pa_t_kernel(tc, mid_logits, x, W2_words, W2_scales, b2, out):
         neg_max = keep.tile([P, TILES], F32)
         exp_sum = keep.tile([P, TILES], F32)
         log_sum = keep.tile([P, TILES], F32)
+        exp_neg_log = keep.tile([P, TILES], F32)
+        ratio = keep.tile([P, TILES], F32)
         shift = keep.tile([P, TILES], F32)
 
         nc.vector.memset(w_scales[:].bitcast(I32), 0)
@@ -178,15 +186,40 @@ def tile_bhcn_awx_pa_t_kernel(tc, mid_logits, x, W2_words, W2_scales, b2, out):
             nc.scalar.activation(
                 out=unread[:], in_=li(t), func=ACT.Exp, bias=neg_max[:, col(t)], accum_out=exp_sum[:, col(t)]
             )
-            if t % LOG_TILES == LOG_TILES - 1:
-                group = slice(t + 1 - LOG_TILES, t + 1)
-                nc.scalar.activation(out=log_sum[:, group], in_=exp_sum[:, group], func=ACT.Ln)
+
+        def group_cols(group):
+            return slice(LOG_TILES * group, LOG_TILES * (group + 1))
+
+        def log_guess(group):
+            cols = group_cols(group)
+            nc.vector.tensor_scalar(
+                out=log_sum[:, cols], in0=exp_sum[:, cols].bitcast(I32),
+                scalar1=GUESS_SCALE, scalar2=GUESS_OFFSET, op0=ALU.mult, op1=ALU.add,
+            )
+
+        def log_exp(group):
+            cols = group_cols(group)
+            nc.scalar.activation(out=exp_neg_log[:, cols], in_=log_sum[:, cols], func=ACT.Exp, scale=-1.0)
+
+        def log_ratio(group):
+            cols = group_cols(group)
+            nc.vector.tensor_tensor(out=ratio[:, cols], in0=exp_neg_log[:, cols], in1=exp_sum[:, cols], op=ALU.mult)
+
+        def log_step(group):
+            cols = group_cols(group)
+            nc.vector.scalar_tensor_tensor(
+                out=log_sum[:, cols], in0=ratio[:, cols], scalar=-1.0, in1=log_sum[:, cols], op0=ALU.add, op1=ALU.add
+            )
+
+        def log_done(group):
+            cols = group_cols(group)
+            nc.vector.tensor_tensor(out=shift[:, cols], in0=neg_max[:, cols], in1=log_sum[:, cols], op=ALU.subtract)
 
         def subtract(t):
-            if t % LOG_TILES == 0:
-                group = slice(t, t + LOG_TILES)
-                nc.vector.tensor_tensor(out=shift[:, group], in0=neg_max[:, group], in1=log_sum[:, group], op=ALU.subtract)
-            nc.vector.tensor_scalar_add(out=li(t), in0=li(t), scalar1=shift[:, col(t)])
+            engine = nc.vector if t >= TILES - LOG_TILES else nc.gpsimd
+            engine.tensor_scalar(
+                out=li(t), in0=li(t), scalar1=1.0, scalar2=shift[:, col(t)], op0=ALU.mult, op1=ALU.add
+            )
             if t % STORE_TILES == STORE_TILES - 1:
                 nc.sync.dma_start(out=out_rows[:, t + 1 - STORE_TILES : t + 1, :], in_=li_pairs[t // STORE_TILES][:])
 
@@ -195,12 +228,24 @@ def tile_bhcn_awx_pa_t_kernel(tc, mid_logits, x, W2_words, W2_scales, b2, out):
                 stage(t)
 
         for turn in range(TILES + LAG_SUBTRACT):
+            group, phase = divmod(turn - LAG_LOG, LOG_TILES)
+            log_runs = 0 <= group < TILES // LOG_TILES
             run(exponentials, turn - LAG_EXP)
+            if log_runs and phase > 0:
+                log_exp(group)
             run(bias_max, turn - LAG_BIAS_MAX)
+            if log_runs and phase == 0:
+                log_guess(group)
+            if log_runs and phase > 0:
+                log_ratio(group)
             run(multiply, turn - LAG_MULTIPLY)
             run(subtract, turn - LAG_SUBTRACT)
             run(transpose, turn - LAG_TRANSPOSE)
             run(normalise, turn - LAG_NORMALISE)
+            if log_runs and phase > 0:
+                log_step(group)
             run(quantise, turn - LAG_QUANTISE)
+            if log_runs and phase == NEWTON_STEPS:
+                log_done(group)
             run(relu_sum, turn)
             run(squares, turn - LAG_SQUARES)

@@ -35,8 +35,9 @@ LAG_NORMALISE = 2
 LAG_TRANSPOSE = 3
 LAG_QUANTISE = 4
 LAG_MULTIPLY = 5
-LAG_BIAS_MAX = 6
-LAG_EXP = 7
+LAG_BIAS = 6
+LAG_MAX = 7
+LAG_EXP = 8
 LAG_LOG = LAG_EXP + LOG_TILES - 1
 LAG_SUBTRACT = LAG_LOG + LOG_TILES
 
@@ -171,12 +172,14 @@ def tile_bhcn_awx_pa_t_kernel(tc, mid_logits, x, W2_words, W2_scales, b2, out):
                     )
                 sums[t].append(acc)
 
-        def bias_max(t):
+        def add_bias(t):
             if t % STORE_TILES == 0:
                 li_pairs[t // STORE_TILES] = logits.tile([P, STORE_TILES, N_OUT], F32, name="li_pair")
             for half, acc in enumerate(sums[t]):
                 cols = slice(BANK * half, BANK * (half + 1))
                 nc.vector.tensor_tensor(out=li(t)[:, cols], in0=acc[:], in1=bias[:, cols], op=ALU.add)
+
+        def row_max(t):
             nc.vector.tensor_reduce(
                 out=neg_max[:, col(t)], in_=li(t), axis=mybir.AxisListType.X, op=ALU.max, negate=True
             )
@@ -233,7 +236,8 @@ def tile_bhcn_awx_pa_t_kernel(tc, mid_logits, x, W2_words, W2_scales, b2, out):
             run(exponentials, turn - LAG_EXP)
             if log_runs and phase > 0:
                 log_exp(group)
-            run(bias_max, turn - LAG_BIAS_MAX)
+            run(add_bias, turn - LAG_BIAS)
+            run(row_max, turn - LAG_MAX)
             if log_runs and phase == 0:
                 log_guess(group)
             if log_runs and phase > 0:

@@ -23,10 +23,9 @@ PASSES = 2
 WORDS = D_HALF // 2
 TILES = ROWS // P
 LOAD_TILES = 4
-STORE_TILES = 2
+LN_EPS = 1e-5
 NEWTON_STEPS = 3
 LOG_TILES = 1 + NEWTON_STEPS
-LN_EPS = 1e-5
 
 FLOPS = 2 * ROWS * (PASSES * D_HALF) * N_OUT
 
@@ -35,9 +34,8 @@ LAG_NORMALISE = 2
 LAG_TRANSPOSE = 3
 LAG_QUANTISE = 4
 LAG_MULTIPLY = 5
-LAG_BIAS = 6
-LAG_MAX = 7
-LAG_EXP = 8
+LAG_BIAS_MAX = 6
+LAG_EXP = 7
 LAG_LOG = LAG_EXP + LOG_TILES - 1
 LAG_SUBTRACT = LAG_LOG + LOG_TILES
 
@@ -55,7 +53,7 @@ def tile_bhcn_awx_pa_t_kernel(tc, mid_logits, x, W2_words, W2_scales, b2, out):
         ctx.enter_context(tc.manual_schedule())
         keep = ctx.enter_context(tc.tile_pool(name="keep", bufs=1))
         work = ctx.enter_context(tc.tile_pool(name="work", bufs=3))
-        logits = ctx.enter_context(tc.tile_pool(name="logits", bufs=7))
+        logits = ctx.enter_context(tc.tile_pool(name="logits", bufs=12))
         psum_t = ctx.enter_context(tc.psum_pool(name="psum_t", bufs=2))
         psum_mm = ctx.enter_context(tc.psum_pool(name="psum_mm", bufs=3))
 
@@ -63,7 +61,9 @@ def tile_bhcn_awx_pa_t_kernel(tc, mid_logits, x, W2_words, W2_scales, b2, out):
         x_sb = keep.tile([P, TILES, D_HALF], BF16)
         w_words = keep.tile([P, PASSES, 2 * N_OUT], U8, align_bytes=64)
         w_scales = keep.tile([P, PASSES, N_OUT], U8, align_bytes=64)
-        bias = keep.tile([P, N_OUT], BF16)
+        bias_row = keep.tile([P, N_OUT], BF16)
+        bias = keep.tile([P, N_OUT], F32)
+        ones = keep.tile([P, P], BF16)
         identity = keep.tile([P, P], F32)
         minus_half = keep.tile([P, 1], F32)
         row_sum = keep.tile([P, TILES], F32)
@@ -78,37 +78,39 @@ def tile_bhcn_awx_pa_t_kernel(tc, mid_logits, x, W2_words, W2_scales, b2, out):
         ratio = keep.tile([P, TILES], F32)
         shift = keep.tile([P, TILES], F32)
 
+        nc.vector.memset(bias_row[:], 0.0)
+        nc.vector.memset(ones[:], 1.0)
         nc.vector.memset(w_scales[:].bitcast(I32), 0)
         nc.vector.memset(minus_half[:], -0.5)
         make_identity(nc, identity[:])
 
-        def load_rows(first):
-            tiles = slice(first, first + LOAD_TILES)
-            nc.sync.dma_start(out=act[:, tiles, :], in_=mid_rows[:, tiles, :])
-            if first == 0:
-                load_weight()
-            nc.sync.dma_start(out=x_sb[:, tiles, :], in_=x_rows[:, tiles, :])
+        def load_rows(tile, rows, first, end):
+            nc.sync.dma_start(out=tile[:, first:end, :], in_=rows[:, first:end, :])
 
-        def load_weight():
-            scale_words = W2_scales.bitcast(I32)
-            for quadrant in range(4):
-                nc.sync.dma_start(
-                    out=w_scales[32 * quadrant : 32 * quadrant + 4, :, :].bitcast(I32),
-                    in_=scale_words[:, 4 * quadrant : 4 * quadrant + 4, :].rearrange("g q w -> q g w"),
-                )
-            nc.sync.dma_start(out=w_words[:].bitcast(I32), in_=W2_words.bitcast(I32).rearrange("g p w -> p g w"))
+        load_rows(act, mid_rows, 0, 1)
+        load_rows(act, mid_rows, 1, LOAD_TILES)
+        load_rows(x_sb, x_rows, 0, LOAD_TILES)
+        nc.sync.dma_start(out=bias_row[0:1, :], in_=b2.unsqueeze(0))
+        nc.sync.dma_start(out=w_words[:].bitcast(I32), in_=W2_words.bitcast(I32).rearrange("g p w -> p g w"))
+        for quadrant in range(4):
+            nc.sync.dma_start(
+                out=w_scales[32 * quadrant : 32 * quadrant + 4, :, :].bitcast(I32),
+                in_=W2_scales.bitcast(I32)[:, 4 * quadrant : 4 * quadrant + 4, :].rearrange("g q w -> q g w"),
+            )
+        for first in range(LOAD_TILES, TILES, LOAD_TILES):
+            load_rows(act, mid_rows, first, first + LOAD_TILES)
+            load_rows(x_sb, x_rows, first, first + LOAD_TILES)
 
-        nc.scalar.dma_start(out=bias[:], in_=b2.partition_broadcast(P))
-        for first in range(0, TILES, LOAD_TILES):
-            load_rows(first)
+        for half in range(N_OUT // BANK):
+            cols = slice(BANK * half, BANK * (half + 1))
+            spread = psum_mm.tile([P, BANK], F32, name="acc%d" % half)
+            nc.tensor.matmul(out=spread[:], lhsT=ones[:], rhs=bias_row[:, cols], start=True, stop=True)
+            nc.vector.tensor_copy(out=bias[:, cols], in_=spread[:])
 
         turned = {}
         codes = {}
         sums = {}
-        li_pairs = {}
-
-        def li(t):
-            return li_pairs[t // STORE_TILES][:, t % STORE_TILES, :]
+        li = {}
 
         def col(t):
             return slice(t, t + 1)
@@ -123,11 +125,12 @@ def tile_bhcn_awx_pa_t_kernel(tc, mid_logits, x, W2_words, W2_scales, b2, out):
         def squares(t):
             unread = work.tile([P, D_HALF], BF16, name="unread_sq")
             nc.scalar.activation(
-                out=unread[:], in_=act[:, t, :], func=ACT.Square, bias=neg_mean[:, col(t)], accum_out=sq_sum[:, col(t)]
+                out=unread[:], in_=act[:, t, :], func=ACT.Square,
+                scale=-float(D_HALF), bias=row_sum[:, col(t)], accum_out=sq_sum[:, col(t)],
             )
             nc.gpsimd.tensor_scalar(
                 out=var_eps[:, col(t)], in0=sq_sum[:, col(t)],
-                scalar1=1.0 / D_HALF, scalar2=LN_EPS, op0=ALU.mult, op1=ALU.add,
+                scalar1=1.0 / D_HALF**3, scalar2=LN_EPS, op0=ALU.mult, op1=ALU.add,
             )
             nc.gpsimd.tensor_tensor(out=inv_std[:, col(t)], in0=var_eps[:, col(t)], in1=minus_half[:], op=ALU.pow)
 
@@ -172,59 +175,47 @@ def tile_bhcn_awx_pa_t_kernel(tc, mid_logits, x, W2_words, W2_scales, b2, out):
                     )
                 sums[t].append(acc)
 
-        def add_bias(t):
-            if t % STORE_TILES == 0:
-                li_pairs[t // STORE_TILES] = logits.tile([P, STORE_TILES, N_OUT], F32, name="li_pair")
+        def bias_max(t):
+            li[t] = logits.tile([P, N_OUT], F32, name="li")
             for half, acc in enumerate(sums[t]):
                 cols = slice(BANK * half, BANK * (half + 1))
-                nc.vector.tensor_tensor(out=li(t)[:, cols], in0=acc[:], in1=bias[:, cols], op=ALU.add)
-
-        def row_max(t):
+                nc.vector.tensor_tensor(out=li[t][:, cols], in0=acc[:], in1=bias[:, cols], op=ALU.add)
             nc.vector.tensor_reduce(
-                out=neg_max[:, col(t)], in_=li(t), axis=mybir.AxisListType.X, op=ALU.max, negate=True
+                out=neg_max[:, col(t)], in_=li[t][:], axis=mybir.AxisListType.X, op=ALU.max, negate=True
             )
 
         def exponentials(t):
             unread = work.tile([P, N_OUT], BF16, name="unread_exp")
             nc.scalar.activation(
-                out=unread[:], in_=li(t), func=ACT.Exp, bias=neg_max[:, col(t)], accum_out=exp_sum[:, col(t)]
+                out=unread[:], in_=li[t][:], func=ACT.Exp, bias=neg_max[:, col(t)], accum_out=exp_sum[:, col(t)]
             )
 
-        def group_cols(group):
-            return slice(LOG_TILES * group, LOG_TILES * (group + 1))
+        def subtract(t):
+            engine = nc.vector if t >= TILES - LOG_TILES else nc.gpsimd
+            engine.tensor_scalar(
+                out=li[t][:], in0=li[t][:], scalar1=1.0, scalar2=shift[:, col(t)], op0=ALU.mult, op1=ALU.add
+            )
+            nc.sync.dma_start(out=out_rows[:, t, :], in_=li[t][:])
 
-        def log_guess(group):
-            cols = group_cols(group)
+        def log_guess(cols):
             nc.vector.tensor_scalar(
                 out=log_sum[:, cols], in0=exp_sum[:, cols].bitcast(I32),
                 scalar1=GUESS_SCALE, scalar2=GUESS_OFFSET, op0=ALU.mult, op1=ALU.add,
             )
 
-        def log_exp(group):
-            cols = group_cols(group)
+        def log_exp(cols):
             nc.scalar.activation(out=exp_neg_log[:, cols], in_=log_sum[:, cols], func=ACT.Exp, scale=-1.0)
 
-        def log_ratio(group):
-            cols = group_cols(group)
+        def log_ratio(cols):
             nc.vector.tensor_tensor(out=ratio[:, cols], in0=exp_neg_log[:, cols], in1=exp_sum[:, cols], op=ALU.mult)
 
-        def log_step(group):
-            cols = group_cols(group)
+        def log_step(cols):
             nc.vector.scalar_tensor_tensor(
                 out=log_sum[:, cols], in0=ratio[:, cols], scalar=-1.0, in1=log_sum[:, cols], op0=ALU.add, op1=ALU.add
             )
 
-        def log_done(group):
-            cols = group_cols(group)
+        def log_done(cols):
             nc.vector.tensor_tensor(out=shift[:, cols], in0=neg_max[:, cols], in1=log_sum[:, cols], op=ALU.subtract)
-
-        def subtract(t):
-            engine = nc.vector if t >= TILES - LOG_TILES else nc.gpsimd
-            engine.tensor_scalar(
-                out=li(t), in0=li(t), scalar1=1.0, scalar2=shift[:, col(t)], op0=ALU.mult, op1=ALU.add
-            )
-            if t % STORE_TILES == STORE_TILES - 1:
-                nc.sync.dma_start(out=out_rows[:, t + 1 - STORE_TILES : t + 1, :], in_=li_pairs[t // STORE_TILES][:])
 
         def run(stage, t):
             if 0 <= t < TILES:
@@ -232,24 +223,28 @@ def tile_bhcn_awx_pa_t_kernel(tc, mid_logits, x, W2_words, W2_scales, b2, out):
 
         for turn in range(TILES + LAG_SUBTRACT):
             group, phase = divmod(turn - LAG_LOG, LOG_TILES)
+            cols = slice(LOG_TILES * group, LOG_TILES * (group + 1))
             log_runs = 0 <= group < TILES // LOG_TILES
+            log_starts = log_runs and phase == 0
+            log_steps = log_runs and phase >= 1
+            log_ends = log_runs and phase == NEWTON_STEPS
+
             run(exponentials, turn - LAG_EXP)
-            if log_runs and phase > 0:
-                log_exp(group)
-            run(add_bias, turn - LAG_BIAS)
-            run(row_max, turn - LAG_MAX)
-            if log_runs and phase == 0:
-                log_guess(group)
-            if log_runs and phase > 0:
-                log_ratio(group)
+            if log_steps:
+                log_exp(cols)
+            run(bias_max, turn - LAG_BIAS_MAX)
+            if log_starts:
+                log_guess(cols)
+            if log_steps:
+                log_ratio(cols)
             run(multiply, turn - LAG_MULTIPLY)
             run(subtract, turn - LAG_SUBTRACT)
             run(transpose, turn - LAG_TRANSPOSE)
             run(normalise, turn - LAG_NORMALISE)
-            if log_runs and phase > 0:
-                log_step(group)
+            if log_steps:
+                log_step(cols)
             run(quantise, turn - LAG_QUANTISE)
-            if log_runs and phase == NEWTON_STEPS:
-                log_done(group)
+            if log_ends:
+                log_done(cols)
             run(relu_sum, turn)
             run(squares, turn - LAG_SQUARES)

@@ -24,8 +24,7 @@ WORDS = D_HALF // 2
 TILES = ROWS // P
 LOAD_TILES = 4
 LN_EPS = 1e-5
-NEWTON_STEPS = 3
-LOG_TILES = 1 + NEWTON_STEPS
+GROUP_SIZES = (4,) * 7 + (3, 1)
 
 FLOPS = 2 * ROWS * (PASSES * D_HALF) * N_OUT
 
@@ -36,11 +35,12 @@ LAG_QUANTISE = 4
 LAG_MULTIPLY = 5
 LAG_BIAS_MAX = 6
 LAG_EXP = 7
-LAG_LOG = LAG_EXP + LOG_TILES - 1
-LAG_SUBTRACT = LAG_LOG + LOG_TILES
+LOG_TURNS = 2
 
 GUESS_SCALE = math.log(2.0) / 2.0**23
 GUESS_OFFSET = math.log(2.0) * (0.043 - 127.0)
+PAID_AT_FIRST = 3.0
+PAID_AT_SECOND = 1.5
 
 
 def tile_bhcn_awx_pa_t_kernel(tc, mid_logits, x, W2_words, W2_scales, b2, out):
@@ -73,9 +73,13 @@ def tile_bhcn_awx_pa_t_kernel(tc, mid_logits, x, W2_words, W2_scales, b2, out):
         inv_std = keep.tile([P, TILES], F32)
         neg_max = keep.tile([P, TILES], F32)
         exp_sum = keep.tile([P, TILES], F32)
-        log_sum = keep.tile([P, TILES], F32)
+        log_guessed = keep.tile([P, TILES], F32)
+        log_better = keep.tile([P, TILES], F32)
         exp_neg_log = keep.tile([P, TILES], F32)
         ratio = keep.tile([P, TILES], F32)
+        factor = keep.tile([P, TILES], F32)
+        gain = keep.tile([P, TILES], F32)
+        rest = keep.tile([P, TILES], F32)
         shift = keep.tile([P, TILES], F32)
 
         nc.vector.memset(bias_row[:], 0.0)
@@ -108,6 +112,7 @@ def tile_bhcn_awx_pa_t_kernel(tc, mid_logits, x, W2_words, W2_scales, b2, out):
             nc.vector.tensor_copy(out=bias[:, cols], in_=spread[:])
 
         turned = {}
+        grouped = {}
         codes = {}
         sums = {}
         li = {}
@@ -147,15 +152,17 @@ def tile_bhcn_awx_pa_t_kernel(tc, mid_logits, x, W2_words, W2_scales, b2, out):
                 for u in range(2):
                     nc.tensor.transpose(turned[t][:, g, u, :], words[:, u:WORDS:2], identity[:])
 
-        def quantise(t):
-            grouped = work.tile([P, PASSES * P * 4], BF16, name="grouped", align_bytes=64)
+        def copy_out(t):
+            grouped[t] = work.tile([P, PASSES * P * 4], BF16, name="grouped", align_bytes=64)
             nc.scalar.copy(
-                out=grouped[:].bitcast(F32).rearrange("p (g r u) -> p g r u", g=PASSES, u=2),
+                out=grouped[t][:].bitcast(F32).rearrange("p (g r u) -> p g r u", g=PASSES, u=2),
                 in_=turned[t][:].rearrange("p g u r -> p g r u"),
             )
+
+        def quantise(t):
             words = work.tile([P, PASSES * P], U32, name="c_words", align_bytes=64)
             plane = work.tile([P, PASSES * P], U8, name="c_scales", align_bytes=64)
-            nc.vector.quantize_mx(out=words[:].bitcast(FP8X4), scales=plane[:], in_=grouped[:])
+            nc.vector.quantize_mx(out=words[:].bitcast(FP8X4), scales=plane[:], in_=grouped[t][:])
             codes[t] = (words, plane)
 
         def multiply(t):
@@ -175,11 +182,13 @@ def tile_bhcn_awx_pa_t_kernel(tc, mid_logits, x, W2_words, W2_scales, b2, out):
                     )
                 sums[t].append(acc)
 
-        def bias_max(t):
-            li[t] = logits.tile([P, N_OUT], F32, name="li")
-            for half, acc in enumerate(sums[t]):
-                cols = slice(BANK * half, BANK * (half + 1))
-                nc.vector.tensor_tensor(out=li[t][:, cols], in0=acc[:], in1=bias[:, cols], op=ALU.add)
+        def add_bias(t, half):
+            if half == 0:
+                li[t] = logits.tile([P, N_OUT], F32, name="li")
+            cols = slice(BANK * half, BANK * (half + 1))
+            nc.vector.tensor_tensor(out=li[t][:, cols], in0=sums[t][half][:], in1=bias[:, cols], op=ALU.add)
+
+        def row_max(t):
             nc.vector.tensor_reduce(
                 out=neg_max[:, col(t)], in_=li[t][:], axis=mybir.AxisListType.X, op=ALU.max, negate=True
             )
@@ -190,61 +199,111 @@ def tile_bhcn_awx_pa_t_kernel(tc, mid_logits, x, W2_words, W2_scales, b2, out):
                 out=unread[:], in_=li[t][:], func=ACT.Exp, bias=neg_max[:, col(t)], accum_out=exp_sum[:, col(t)]
             )
 
-        def subtract(t):
-            engine = nc.vector if t >= TILES - LOG_TILES else nc.gpsimd
-            engine.tensor_scalar(
-                out=li[t][:], in0=li[t][:], scalar1=1.0, scalar2=shift[:, col(t)], op0=ALU.mult, op1=ALU.add
-            )
-            nc.sync.dma_start(out=out_rows[:, t, :], in_=li[t][:])
+        def subtract(t, who):
+            if who == "scalar":
+                nc.scalar.activation(out=li[t][:], in_=li[t][:], func=ACT.Identity, bias=shift[:, col(t)], scale=1.0)
+                nc.scalar.dma_start(out=out_rows[:, t, :], in_=li[t][:])
+            else:
+                engine = nc.vector if who == "vector" else nc.gpsimd
+                engine.tensor_scalar(
+                    out=li[t][:], in0=li[t][:], scalar1=1.0, scalar2=shift[:, col(t)], op0=ALU.mult, op1=ALU.add
+                )
+                nc.sync.dma_start(out=out_rows[:, t, :], in_=li[t][:])
 
         def log_guess(cols):
             nc.vector.tensor_scalar(
-                out=log_sum[:, cols], in0=exp_sum[:, cols].bitcast(I32),
-                scalar1=GUESS_SCALE, scalar2=GUESS_OFFSET, op0=ALU.mult, op1=ALU.add,
+                out=log_guessed[:, cols], in0=exp_sum[:, cols].bitcast(I32),
+                scalar1=GUESS_SCALE, scalar2=GUESS_OFFSET - PAID_AT_FIRST, op0=ALU.mult, op1=ALU.add,
             )
 
-        def log_exp(cols):
-            nc.scalar.activation(out=exp_neg_log[:, cols], in_=log_sum[:, cols], func=ACT.Exp, scale=-1.0)
+        def log_exp_first(cols):
+            nc.scalar.activation(
+                out=exp_neg_log[:, cols], in_=log_guessed[:, cols], func=ACT.Exp, scale=-1.0, bias=-PAID_AT_FIRST
+            )
+
+        def log_exp_second(cols):
+            nc.scalar.activation(
+                out=exp_neg_log[:, cols], in_=log_better[:, cols], func=ACT.Exp, scale=-1.0, bias=-PAID_AT_SECOND
+            )
 
         def log_ratio(cols):
             nc.vector.tensor_tensor(out=ratio[:, cols], in0=exp_neg_log[:, cols], in1=exp_sum[:, cols], op=ALU.mult)
 
-        def log_step(cols):
-            nc.vector.scalar_tensor_tensor(
-                out=log_sum[:, cols], in0=ratio[:, cols], scalar=-1.0, in1=log_sum[:, cols], op0=ALU.add, op1=ALU.add
+        def log_factor(cols):
+            nc.vector.tensor_scalar(
+                out=factor[:, cols], in0=ratio[:, cols], scalar1=-0.5, scalar2=2.0, op0=ALU.mult, op1=ALU.add
             )
 
-        def log_done(cols):
-            nc.vector.tensor_tensor(out=shift[:, cols], in0=neg_max[:, cols], in1=log_sum[:, cols], op=ALU.subtract)
+        def log_gain(cols):
+            nc.vector.tensor_tensor(out=gain[:, cols], in0=factor[:, cols], in1=ratio[:, cols], op=ALU.mult)
 
-        def run(stage, t):
+        def log_first_step(cols):
+            nc.vector.tensor_tensor(out=log_better[:, cols], in0=log_guessed[:, cols], in1=gain[:, cols], op=ALU.add)
+
+        def log_rest(cols):
+            nc.vector.tensor_tensor(out=rest[:, cols], in0=neg_max[:, cols], in1=log_better[:, cols], op=ALU.subtract)
+
+        def log_shift(cols):
+            nc.vector.tensor_tensor(out=shift[:, cols], in0=rest[:, cols], in1=gain[:, cols], op=ALU.subtract)
+
+        def run(stage, t, *more):
             if 0 <= t < TILES:
-                stage(t)
+                stage(t, *more)
 
-        for turn in range(TILES + LAG_SUBTRACT):
-            group, phase = divmod(turn - LAG_LOG, LOG_TILES)
-            cols = slice(LOG_TILES * group, LOG_TILES * (group + 1))
-            log_runs = 0 <= group < TILES // LOG_TILES
-            log_starts = log_runs and phase == 0
-            log_steps = log_runs and phase >= 1
-            log_ends = log_runs and phase == NEWTON_STEPS
+        VECTOR_PIECES = (
+            (0, 2, log_guess),
+            (1, 0, log_ratio), (1, 1, log_factor), (1, 2, log_gain), (1, 3, log_first_step), (1, 4, log_rest),
+            (2, 0, log_ratio), (2, 1, log_factor), (2, 2, log_gain), (2, 3, log_shift),
+        )
+        SCALAR_PIECES = ((0, log_exp_first), (1, log_exp_second))
+        in_gap = {}
+        at_end = {}
+        ready = {}
+        first = 0
+        for size in GROUP_SIZES:
+            cols = slice(first, first + size)
+            start = first + size - 1 + LAG_EXP
+            for later, gap, piece in VECTOR_PIECES:
+                in_gap.setdefault((start + later, gap), []).append((piece, cols))
+            for later, piece in SCALAR_PIECES:
+                at_end.setdefault(start + later, []).append((piece, cols))
+            ready[max(start + LOG_TURNS, min(start + LOG_TURNS + 1, TILES + LAG_SQUARES))] = list(range(first, first + size))
+            first += size
+        assert first == TILES
 
+        def pieces(found):
+            for piece, cols in found:
+                piece(cols)
+
+        LAST_SQUARES_TURN = TILES - 1 + LAG_SQUARES
+        LAST_MAX_TURN = TILES - 1 + LAG_BIAS_MAX
+        waiting = []
+        for turn in range(TILES + LAG_EXP + LOG_TURNS + 1):
             run(exponentials, turn - LAG_EXP)
-            if log_steps:
-                log_exp(cols)
-            run(bias_max, turn - LAG_BIAS_MAX)
-            if log_starts:
-                log_guess(cols)
-            if log_steps:
-                log_ratio(cols)
+            run(copy_out, turn - LAG_QUANTISE)
+            run(add_bias, turn - LAG_BIAS_MAX, 0)
+            pieces(in_gap.get((turn, 0), []))
+            run(add_bias, turn - LAG_BIAS_MAX, 1)
+            pieces(in_gap.get((turn, 1), []))
+            run(row_max, turn - LAG_BIAS_MAX)
+            pieces(in_gap.get((turn, 2), []))
             run(multiply, turn - LAG_MULTIPLY)
-            run(subtract, turn - LAG_SUBTRACT)
             run(transpose, turn - LAG_TRANSPOSE)
             run(normalise, turn - LAG_NORMALISE)
-            if log_steps:
-                log_step(cols)
+            pieces(in_gap.get((turn, 3), []))
+            waiting.extend(ready.get(turn, []))
+            if turn > LAST_MAX_TURN:
+                takers = ("vector", "gpsimd")
+            elif LAST_SQUARES_TURN < turn < LAST_MAX_TURN:
+                takers = ("gpsimd", "scalar")
+            else:
+                takers = ("gpsimd",)
+            for who in takers:
+                if waiting:
+                    subtract(waiting.pop(0), who)
             run(quantise, turn - LAG_QUANTISE)
-            if log_ends:
-                log_done(cols)
+            pieces(in_gap.get((turn, 4), []))
             run(relu_sum, turn)
             run(squares, turn - LAG_SQUARES)
+            pieces(at_end.get(turn, []))
+        assert not waiting

@@ -24,7 +24,10 @@ WORDS = D_HALF // 2
 TILES = ROWS // P
 LOAD_TILES = 4
 LN_EPS = 1e-5
-GROUP_SIZES = (4,) * 7 + (3, 1)
+GROUP_SIZES = (8,) * 3 + (4, 3, 1)
+NORM_GROUPS = (2,) * 16
+LEAD = 2
+HEAD_TILES = 2
 
 FLOPS = 2 * ROWS * (PASSES * D_HALF) * N_OUT
 
@@ -53,7 +56,7 @@ def tile_bhcn_awx_pa_t_kernel(tc, mid_logits, x, W2_words, W2_scales, b2, out):
         ctx.enter_context(tc.manual_schedule())
         keep = ctx.enter_context(tc.tile_pool(name="keep", bufs=1))
         work = ctx.enter_context(tc.tile_pool(name="work", bufs=3))
-        logits = ctx.enter_context(tc.tile_pool(name="logits", bufs=12))
+        logits = ctx.enter_context(tc.tile_pool(name="logits", bufs=16))
         psum_t = ctx.enter_context(tc.psum_pool(name="psum_t", bufs=2))
         psum_mm = ctx.enter_context(tc.psum_pool(name="psum_mm", bufs=3))
 
@@ -65,7 +68,7 @@ def tile_bhcn_awx_pa_t_kernel(tc, mid_logits, x, W2_words, W2_scales, b2, out):
         bias = keep.tile([P, N_OUT], F32)
         ones = keep.tile([P, P], BF16)
         identity = keep.tile([P, P], F32)
-        minus_half = keep.tile([P, 1], F32)
+        minus_half = keep.tile([P, max(NORM_GROUPS)], F32)
         row_sum = keep.tile([P, TILES], F32)
         neg_mean = keep.tile([P, TILES], F32)
         sq_sum = keep.tile([P, TILES], F32)
@@ -116,16 +119,13 @@ def tile_bhcn_awx_pa_t_kernel(tc, mid_logits, x, W2_words, W2_scales, b2, out):
         codes = {}
         sums = {}
         li = {}
+        norm_after = {}
 
         def col(t):
             return slice(t, t + 1)
 
         def relu_sum(t):
             nc.scalar.activation(out=act[:, t, :], in_=act[:, t, :], func=ACT.Relu, accum_out=row_sum[:, col(t)])
-            nc.gpsimd.tensor_scalar(
-                out=neg_mean[:, col(t)], in0=row_sum[:, col(t)],
-                scalar1=-1.0 / D_HALF, scalar2=0.0, op0=ALU.mult, op1=ALU.add,
-            )
 
         def squares(t):
             unread = work.tile([P, D_HALF], BF16, name="unread_sq")
@@ -133,11 +133,21 @@ def tile_bhcn_awx_pa_t_kernel(tc, mid_logits, x, W2_words, W2_scales, b2, out):
                 out=unread[:], in_=act[:, t, :], func=ACT.Square,
                 scale=-float(D_HALF), bias=row_sum[:, col(t)], accum_out=sq_sum[:, col(t)],
             )
+            if t in norm_after:
+                norm_scalars(norm_after[t])
+
+        def norm_scalars(cols):
             nc.gpsimd.tensor_scalar(
-                out=var_eps[:, col(t)], in0=sq_sum[:, col(t)],
+                out=neg_mean[:, cols], in0=row_sum[:, cols],
+                scalar1=-1.0 / D_HALF, scalar2=0.0, op0=ALU.mult, op1=ALU.add,
+            )
+            nc.gpsimd.tensor_scalar(
+                out=var_eps[:, cols], in0=sq_sum[:, cols],
                 scalar1=1.0 / D_HALF**3, scalar2=LN_EPS, op0=ALU.mult, op1=ALU.add,
             )
-            nc.gpsimd.tensor_tensor(out=inv_std[:, col(t)], in0=var_eps[:, col(t)], in1=minus_half[:], op=ALU.pow)
+            nc.gpsimd.tensor_tensor(
+                out=inv_std[:, cols], in0=var_eps[:, cols], in1=minus_half[:, 0 : cols.stop - cols.start], op=ALU.pow
+            )
 
         def normalise(t):
             nc.vector.tensor_scalar(
@@ -154,7 +164,8 @@ def tile_bhcn_awx_pa_t_kernel(tc, mid_logits, x, W2_words, W2_scales, b2, out):
 
         def copy_out(t):
             grouped[t] = work.tile([P, PASSES * P * 4], BF16, name="grouped", align_bytes=64)
-            nc.scalar.copy(
+            copy = nc.vector.tensor_copy if t < HEAD_TILES else nc.scalar.copy
+            copy(
                 out=grouped[t][:].bitcast(F32).rearrange("p (g r u) -> p g r u", g=PASSES, u=2),
                 in_=turned[t][:].rearrange("p g u r -> p g r u"),
             )
@@ -246,6 +257,15 @@ def tile_bhcn_awx_pa_t_kernel(tc, mid_logits, x, W2_words, W2_scales, b2, out):
         def log_shift(cols):
             nc.vector.tensor_tensor(out=shift[:, cols], in0=rest[:, cols], in1=gain[:, cols], op=ALU.subtract)
 
+        upstream = []
+        first = 0
+        for size in NORM_GROUPS:
+            upstream.extend([(relu_sum, t) for t in range(first, first + size)])
+            upstream.extend([(squares, t) for t in range(first, first + size)])
+            norm_after[first + size - 1] = slice(first, first + size)
+            first += size
+        assert first == TILES
+
         def run(stage, t, *more):
             if 0 <= t < TILES:
                 stage(t, *more)
@@ -267,7 +287,8 @@ def tile_bhcn_awx_pa_t_kernel(tc, mid_logits, x, W2_words, W2_scales, b2, out):
                 in_gap.setdefault((start + later, gap), []).append((piece, cols))
             for later, piece in SCALAR_PIECES:
                 at_end.setdefault(start + later, []).append((piece, cols))
-            ready[max(start + LOG_TURNS, min(start + LOG_TURNS + 1, TILES + LAG_SQUARES))] = list(range(first, first + size))
+            begin = max(start + LOG_TURNS, min(start + LOG_TURNS + 1, (2 * TILES - LEAD) // 2))
+            ready.setdefault(begin, []).extend(range(first, first + size))
             first += size
         assert first == TILES
 
@@ -275,8 +296,10 @@ def tile_bhcn_awx_pa_t_kernel(tc, mid_logits, x, W2_words, W2_scales, b2, out):
             for piece, cols in found:
                 piece(cols)
 
-        LAST_SQUARES_TURN = TILES - 1 + LAG_SQUARES
+        LAST_SQUARES_TURN = (2 * TILES - LEAD) // 2 - 1
         LAST_MAX_TURN = TILES - 1 + LAG_BIAS_MAX
+        for stage, t in upstream[:LEAD]:
+            stage(t)
         waiting = []
         for turn in range(TILES + LAG_EXP + LOG_TURNS + 1):
             run(exponentials, turn - LAG_EXP)
@@ -293,7 +316,7 @@ def tile_bhcn_awx_pa_t_kernel(tc, mid_logits, x, W2_words, W2_scales, b2, out):
             pieces(in_gap.get((turn, 3), []))
             waiting.extend(ready.get(turn, []))
             if turn > LAST_MAX_TURN:
-                takers = ("vector", "gpsimd")
+                takers = ("vector", "vector")
             elif LAST_SQUARES_TURN < turn < LAST_MAX_TURN:
                 takers = ("gpsimd", "scalar")
             else:
@@ -303,7 +326,7 @@ def tile_bhcn_awx_pa_t_kernel(tc, mid_logits, x, W2_words, W2_scales, b2, out):
                     subtract(waiting.pop(0), who)
             run(quantise, turn - LAG_QUANTISE)
             pieces(in_gap.get((turn, 4), []))
-            run(relu_sum, turn)
-            run(squares, turn - LAG_SQUARES)
+            for stage, t in upstream[LEAD + 2 * turn : LEAD + 2 * turn + 2]:
+                stage(t)
             pieces(at_end.get(turn, []))
         assert not waiting

@@ -126,6 +126,12 @@ def tile_bhcn_awx_pa_t_kernel(tc, mid_logits, x, W2_words, W2_scales, b2, out):
 
         def relu_sum(t):
             nc.scalar.activation(out=act[:, t, :], in_=act[:, t, :], func=ACT.Relu, accum_out=row_sum[:, col(t)])
+            if t in norm_after:
+                cols = norm_after[t]
+                nc.gpsimd.tensor_scalar(
+                    out=neg_mean[:, cols], in0=row_sum[:, cols],
+                    scalar1=-1.0 / D_HALF, scalar2=0.0, op0=ALU.mult, op1=ALU.add,
+                )
 
         def squares(t):
             unread = work.tile([P, D_HALF], BF16, name="unread_sq")
@@ -137,10 +143,6 @@ def tile_bhcn_awx_pa_t_kernel(tc, mid_logits, x, W2_words, W2_scales, b2, out):
                 norm_scalars(norm_after[t])
 
         def norm_scalars(cols):
-            nc.gpsimd.tensor_scalar(
-                out=neg_mean[:, cols], in0=row_sum[:, cols],
-                scalar1=-1.0 / D_HALF, scalar2=0.0, op0=ALU.mult, op1=ALU.add,
-            )
             nc.gpsimd.tensor_scalar(
                 out=var_eps[:, cols], in0=sq_sum[:, cols],
                 scalar1=1.0 / D_HALF**3, scalar2=LN_EPS, op0=ALU.mult, op1=ALU.add,

@@ -37,7 +37,8 @@ LAG_TRANSPOSE = 3
 LAG_QUANTISE = 4
 LAG_MULTIPLY = 5
 LAG_BIAS_MAX = 6
-LAG_EXP = 7
+LAG_MAX = 7
+LAG_EXP = 8
 LOG_TURNS = 2
 
 GUESS_SCALE = math.log(2.0) / 2.0**23
@@ -56,7 +57,7 @@ def tile_bhcn_awx_pa_t_kernel(tc, mid_logits, x, W2_words, W2_scales, b2, out):
         ctx.enter_context(tc.manual_schedule())
         keep = ctx.enter_context(tc.tile_pool(name="keep", bufs=1))
         work = ctx.enter_context(tc.tile_pool(name="work", bufs=3))
-        logits = ctx.enter_context(tc.tile_pool(name="logits", bufs=16))
+        logits = ctx.enter_context(tc.tile_pool(name="logits", bufs=17))
         psum_t = ctx.enter_context(tc.psum_pool(name="psum_t", bufs=2))
         psum_mm = ctx.enter_context(tc.psum_pool(name="psum_mm", bufs=3))
 
@@ -299,7 +300,7 @@ def tile_bhcn_awx_pa_t_kernel(tc, mid_logits, x, W2_words, W2_scales, b2, out):
                 piece(cols)
 
         LAST_SQUARES_TURN = (2 * TILES - LEAD) // 2 - 1
-        LAST_MAX_TURN = TILES - 1 + LAG_BIAS_MAX
+        LAST_MAX_TURN = TILES - 1 + LAG_MAX
         for stage, t in upstream[:LEAD]:
             stage(t)
         waiting = []
@@ -308,9 +309,9 @@ def tile_bhcn_awx_pa_t_kernel(tc, mid_logits, x, W2_words, W2_scales, b2, out):
             run(copy_out, turn - LAG_QUANTISE)
             run(add_bias, turn - LAG_BIAS_MAX, 0)
             pieces(in_gap.get((turn, 0), []))
-            run(add_bias, turn - LAG_BIAS_MAX, 1)
+            run(row_max, turn - LAG_MAX)
             pieces(in_gap.get((turn, 1), []))
-            run(row_max, turn - LAG_BIAS_MAX)
+            run(add_bias, turn - LAG_BIAS_MAX, 1)
             pieces(in_gap.get((turn, 2), []))
             run(multiply, turn - LAG_MULTIPLY)
             run(transpose, turn - LAG_TRANSPOSE)

@@ -43,8 +43,8 @@ LOG_TURNS = 2
 
 GUESS_SCALE = math.log(2.0) / 2.0**23
 GUESS_OFFSET = math.log(2.0) * (0.043 - 127.0)
-PAID_AT_FIRST = 3.0
-PAID_AT_SECOND = 1.5
+AHEAD_AT_FIRST = 1.0
+AHEAD_AT_SECOND = 0.5
 
 
 def tile_bhcn_awx_pa_t_kernel(tc, mid_logits, x, W2_words, W2_scales, b2, out):
@@ -81,8 +81,7 @@ def tile_bhcn_awx_pa_t_kernel(tc, mid_logits, x, W2_words, W2_scales, b2, out):
         log_better = keep.tile([P, TILES], F32)
         exp_neg_log = keep.tile([P, TILES], F32)
         ratio = keep.tile([P, TILES], F32)
-        factor = keep.tile([P, TILES], F32)
-        gain = keep.tile([P, TILES], F32)
+        square = keep.tile([P, TILES], F32)
         rest = keep.tile([P, TILES], F32)
         shift = keep.tile([P, TILES], F32)
 
@@ -227,38 +226,38 @@ def tile_bhcn_awx_pa_t_kernel(tc, mid_logits, x, W2_words, W2_scales, b2, out):
         def log_guess(cols):
             nc.vector.tensor_scalar(
                 out=log_guessed[:, cols], in0=exp_sum[:, cols].bitcast(I32),
-                scalar1=GUESS_SCALE, scalar2=GUESS_OFFSET - PAID_AT_FIRST, op0=ALU.mult, op1=ALU.add,
+                scalar1=GUESS_SCALE, scalar2=GUESS_OFFSET + AHEAD_AT_FIRST, op0=ALU.mult, op1=ALU.add,
             )
 
         def log_exp_first(cols):
             nc.scalar.activation(
-                out=exp_neg_log[:, cols], in_=log_guessed[:, cols], func=ACT.Exp, scale=-1.0, bias=-PAID_AT_FIRST
+                out=exp_neg_log[:, cols], in_=log_guessed[:, cols], func=ACT.Exp, scale=-1.0, bias=AHEAD_AT_FIRST
             )
 
         def log_exp_second(cols):
             nc.scalar.activation(
-                out=exp_neg_log[:, cols], in_=log_better[:, cols], func=ACT.Exp, scale=-1.0, bias=-PAID_AT_SECOND
+                out=exp_neg_log[:, cols], in_=log_better[:, cols], func=ACT.Exp, scale=-1.0, bias=AHEAD_AT_SECOND
             )
 
         def log_ratio(cols):
             nc.vector.tensor_tensor(out=ratio[:, cols], in0=exp_neg_log[:, cols], in1=exp_sum[:, cols], op=ALU.mult)
 
-        def log_factor(cols):
-            nc.vector.tensor_scalar(
-                out=factor[:, cols], in0=ratio[:, cols], scalar1=-0.5, scalar2=2.0, op0=ALU.mult, op1=ALU.add
-            )
-
-        def log_gain(cols):
-            nc.vector.tensor_tensor(out=gain[:, cols], in0=factor[:, cols], in1=ratio[:, cols], op=ALU.mult)
+        def log_square(cols):
+            nc.scalar.activation(out=square[:, cols], in_=ratio[:, cols], func=ACT.Square, scale=0.5, bias=-1.0)
 
         def log_first_step(cols):
-            nc.vector.tensor_tensor(out=log_better[:, cols], in0=log_guessed[:, cols], in1=gain[:, cols], op=ALU.add)
+            nc.vector.scalar_tensor_tensor(
+                out=log_better[:, cols], in0=square[:, cols], scalar=-2.0, in1=log_guessed[:, cols],
+                op0=ALU.mult, op1=ALU.add,
+            )
 
         def log_rest(cols):
             nc.vector.tensor_tensor(out=rest[:, cols], in0=neg_max[:, cols], in1=log_better[:, cols], op=ALU.subtract)
 
         def log_shift(cols):
-            nc.vector.tensor_tensor(out=shift[:, cols], in0=rest[:, cols], in1=gain[:, cols], op=ALU.subtract)
+            nc.vector.scalar_tensor_tensor(
+                out=shift[:, cols], in0=square[:, cols], scalar=2.0, in1=rest[:, cols], op0=ALU.mult, op1=ALU.add
+            )
 
         upstream = []
         first = 0
@@ -275,12 +274,14 @@ def tile_bhcn_awx_pa_t_kernel(tc, mid_logits, x, W2_words, W2_scales, b2, out):
 
         VECTOR_PIECES = (
             (0, 2, log_guess),
-            (1, 0, log_ratio), (1, 1, log_factor), (1, 2, log_gain), (1, 3, log_first_step), (1, 4, log_rest),
-            (2, 0, log_ratio), (2, 1, log_factor), (2, 2, log_gain), (2, 3, log_shift),
+            (1, 0, log_ratio), (1, 3, log_first_step), (1, 4, log_rest),
+            (2, 0, log_ratio), (2, 3, log_shift),
         )
         SCALAR_PIECES = ((0, log_exp_first), (1, log_exp_second))
+        SCALAR_SQUARES = (1, 2)
         in_gap = {}
         at_end = {}
+        in_middle = {}
         ready = {}
         first = 0
         for size in GROUP_SIZES:
@@ -290,6 +291,8 @@ def tile_bhcn_awx_pa_t_kernel(tc, mid_logits, x, W2_words, W2_scales, b2, out):
                 in_gap.setdefault((start + later, gap), []).append((piece, cols))
             for later, piece in SCALAR_PIECES:
                 at_end.setdefault(start + later, []).append((piece, cols))
+            for later in SCALAR_SQUARES:
+                in_middle.setdefault(start + later, []).append((log_square, cols))
             begin = max(start + LOG_TURNS, min(start + LOG_TURNS + 1, (2 * TILES - LEAD) // 2))
             ready.setdefault(begin, []).extend(range(first, first + size))
             first += size
@@ -309,6 +312,7 @@ def tile_bhcn_awx_pa_t_kernel(tc, mid_logits, x, W2_words, W2_scales, b2, out):
             run(copy_out, turn - LAG_QUANTISE)
             run(add_bias, turn - LAG_BIAS_MAX, 0)
             pieces(in_gap.get((turn, 0), []))
+            pieces(in_middle.get(turn, []))
             run(row_max, turn - LAG_MAX)
             pieces(in_gap.get((turn, 1), []))
             run(add_bias, turn - LAG_BIAS_MAX, 1)

@@ -24,7 +24,7 @@ WORDS = D_HALF // 2
 TILES = ROWS // P
 LOAD_TILES = 4
 LN_EPS = 1e-5
-GROUP_SIZES = (8,) * 3 + (4, 3, 1)
+GROUP_SIZES = (8,) * 3 + (4, 4)
 NORM_GROUPS = (2,) * 16
 LEAD = 2
 HEAD_TILES = 2
@@ -166,7 +166,7 @@ def tile_bhcn_awx_pa_t_kernel(tc, mid_logits, x, W2_words, W2_scales, b2, out):
 
         def copy_out(t):
             grouped[t] = work.tile([P, PASSES * P * 4], BF16, name="grouped", align_bytes=64)
-            copy = nc.vector.tensor_copy if t < HEAD_TILES else nc.scalar.copy
+            copy = nc.vector.tensor_copy if t < HEAD_TILES or t % 8 == 0 else nc.scalar.copy
             copy(
                 out=grouped[t][:].bitcast(F32).rearrange("p (g r u) -> p g r u", g=PASSES, u=2),
                 in_=turned[t][:].rearrange("p g u r -> p g r u"),
@@ -329,7 +329,7 @@ def tile_bhcn_awx_pa_t_kernel(tc, mid_logits, x, W2_words, W2_scales, b2, out):
             else:
                 takers = ("gpsimd",)
             for who in takers:
-                if waiting:
+                if waiting and not (who == "scalar" and waiting[0] in ready.get(turn, [])):
                     subtract(waiting.pop(0), who)
             run(quantise, turn - LAG_QUANTISE)
             pieces(in_gap.get((turn, 4), []))

import math
from contextlib import ExitStack

import concourse.mybir as mybir
from concourse.masks import make_identity

F32 = mybir.dt.float32
BF16 = mybir.dt.bfloat16
I32 = mybir.dt.int32
U32 = mybir.dt.uint32
U8 = mybir.dt.uint8
FP8X4 = mybir.dt.float8_e4m3fn_x4
FP4X4 = mybir.dt.float4_e2m1fn_x4
ACT = mybir.ActivationFunctionType
ALU = mybir.AluOpType

P = 128
ROWS = 4096
D_HALF = 512
N_OUT = 1024
BANK = 512
PASSES = 2
WORDS = D_HALF // 2
TILES = ROWS // P
LOAD_TILES = 4
LN_EPS = 1e-5
GROUP_SIZES = (8,) * 3 + (4, 4)
NORM_GROUPS = (2,) * 16
LEAD = 2
HEAD_TILES = 2

FLOPS = 2 * ROWS * (PASSES * D_HALF) * N_OUT

LAG_SQUARES = 1
LAG_NORMALISE = 2
LAG_TRANSPOSE = 3
LAG_QUANTISE = 4
LAG_MULTIPLY = 5
LAG_BIAS_MAX = 6
LAG_MAX = 7
LAG_EXP = 8
LOG_TURNS = 2

GUESS_SCALE = math.log(2.0) / 2.0**23
GUESS_OFFSET = math.log(2.0) * (0.043 - 127.0)
AHEAD_AT_FIRST = 1.0
AHEAD_AT_SECOND = 0.5


def tile_bhcn_awx_pa_t_kernel(tc, mid_logits, x, W2_words, W2_scales, b2, out):
    nc = tc.nc
    mid_rows = mid_logits.rearrange("(p t) k -> p t k", t=TILES)
    x_rows = x.rearrange("(p t) k -> p t k", t=TILES)
    out_rows = out.rearrange("(p t) n -> p t n", t=TILES)

    with ExitStack() as ctx:
        ctx.enter_context(tc.manual_schedule())
        keep = ctx.enter_context(tc.tile_pool(name="keep", bufs=1))
        work = ctx.enter_context(tc.tile_pool(name="work", bufs=3))
        logits = ctx.enter_context(tc.tile_pool(name="logits", bufs=17))
        psum_t = ctx.enter_context(tc.psum_pool(name="psum_t", bufs=2))
        psum_mm = ctx.enter_context(tc.psum_pool(name="psum_mm", bufs=3))

        act = keep.tile([P, TILES, D_HALF], BF16)
        x_sb = keep.tile([P, TILES, D_HALF], BF16)
        w_words = keep.tile([P, PASSES, 2 * N_OUT], U8, align_bytes=64)
        w_scales = keep.tile([P, PASSES, N_OUT], U8, align_bytes=64)
        bias_row = keep.tile([P, N_OUT], BF16)
        bias = keep.tile([P, N_OUT], F32)
        ones = keep.tile([P, P], BF16)
        identity = keep.tile([P, P], F32)
        minus_half = keep.tile([P, max(NORM_GROUPS)], F32)
        row_sum = keep.tile([P, TILES], F32)
        neg_mean = keep.tile([P, TILES], F32)
        sq_sum = keep.tile([P, TILES], F32)
        var_eps = keep.tile([P, TILES], F32)
        inv_std = keep.tile([P, TILES], F32)
        neg_max = keep.tile([P, TILES], F32)
        exp_sum = keep.tile([P, TILES], F32)
        log_guessed = keep.tile([P, TILES], F32)
        log_better = keep.tile([P, TILES], F32)
        exp_neg_log = keep.tile([P, TILES], F32)
        ratio = keep.tile([P, TILES], F32)
        square = keep.tile([P, TILES], F32)
        rest = keep.tile([P, TILES], F32)
        shift = keep.tile([P, TILES], F32)

        nc.vector.memset(bias_row[:], 0.0)
        nc.vector.memset(ones[:], 1.0)
        nc.vector.memset(w_scales[:].bitcast(I32), 0)
        nc.vector.memset(minus_half[:], -0.5)
        make_identity(nc, identity[:])

        def load_rows(tile, rows, first, end):
            nc.sync.dma_start(out=tile[:, first:end, :], in_=rows[:, first:end, :])

        load_rows(act, mid_rows, 0, 1)
        load_rows(act, mid_rows, 1, LOAD_TILES)
        load_rows(x_sb, x_rows, 0, LOAD_TILES)
        nc.sync.dma_start(out=bias_row[0:1, :], in_=b2.unsqueeze(0))
        nc.sync.dma_start(out=w_words[:].bitcast(I32), in_=W2_words.bitcast(I32).rearrange("g p w -> p g w"))
        for quadrant in range(4):
            nc.sync.dma_start(
                out=w_scales[32 * quadrant : 32 * quadrant + 4, :, :].bitcast(I32),
                in_=W2_scales.bitcast(I32)[:, 4 * quadrant : 4 * quadrant + 4, :].rearrange("g q w -> q g w"),
            )
        for first in range(LOAD_TILES, TILES, LOAD_TILES):
            load_rows(act, mid_rows, first, first + LOAD_TILES)
            load_rows(x_sb, x_rows, first, first + LOAD_TILES)

        for half in range(N_OUT // BANK):
            cols = slice(BANK * half, BANK * (half + 1))
            spread = psum_mm.tile([P, BANK], F32, name="acc%d" % half)
            nc.tensor.matmul(out=spread[:], lhsT=ones[:], rhs=bias_row[:, cols], start=True, stop=True)
            nc.vector.tensor_copy(out=bias[:, cols], in_=spread[:])

        turned = {}
        grouped = {}
        codes = {}
        sums = {}
        li = {}
        norm_after = {}

        def col(t):
            return slice(t, t + 1)

        def relu_sum(t):
            nc.scalar.activation(out=act[:, t, :], in_=act[:, t, :], func=ACT.Relu, accum_out=row_sum[:, col(t)])
            if t in norm_after:
                cols = norm_after[t]
                nc.gpsimd.tensor_scalar(
                    out=neg_mean[:, cols], in0=row_sum[:, cols],
                    scalar1=-1.0 / D_HALF, scalar2=0.0, op0=ALU.mult, op1=ALU.add,
                )

        def squares(t):
            unread = work.tile([P, D_HALF], BF16, name="unread_sq")
            nc.scalar.activation(
                out=unread[:], in_=act[:, t, :], func=ACT.Square,
                scale=-float(D_HALF), bias=row_sum[:, col(t)], accum_out=sq_sum[:, col(t)],
            )
            if t in norm_after:
                norm_scalars(norm_after[t])

        def norm_scalars(cols):
            nc.gpsimd.tensor_scalar(
                out=var_eps[:, cols], in0=sq_sum[:, cols],
                scalar1=1.0 / D_HALF**3, scalar2=LN_EPS, op0=ALU.mult, op1=ALU.add,
            )
            nc.gpsimd.tensor_tensor(
                out=inv_std[:, cols], in0=var_eps[:, cols], in1=minus_half[:, 0 : cols.stop - cols.start], op=ALU.pow
            )

        def normalise(t):
            nc.vector.tensor_scalar(
                out=act[:, t, :], in0=act[:, t, :],
                scalar1=neg_mean[:, col(t)], scalar2=inv_std[:, col(t)], op0=ALU.add, op1=ALU.mult,
            )

        def transpose(t):
            turned[t] = psum_t.tile([P, PASSES, 2, P], F32, name="turned")
            for g, rows in enumerate((act, x_sb)):
                words = rows[:, t, :].bitcast(F32)
                for u in range(2):
                    nc.tensor.transpose(turned[t][:, g, u, :], words[:, u:WORDS:2], identity[:])

        def copy_out(t):
            grouped[t] = work.tile([P, PASSES * P * 4], BF16, name="grouped", align_bytes=64)
            copy = nc.vector.tensor_copy if t < HEAD_TILES or t % 8 == 0 else nc.scalar.copy
            copy(
                out=grouped[t][:].bitcast(F32).rearrange("p (g r u) -> p g r u", g=PASSES, u=2),
                in_=turned[t][:].rearrange("p g u r -> p g r u"),
            )

        def quantise(t):
            words = work.tile([P, PASSES * P], U32, name="c_words", align_bytes=64)
            plane = work.tile([P, PASSES * P], U8, name="c_scales", align_bytes=64)
            nc.vector.quantize_mx(out=words[:].bitcast(FP8X4), scales=plane[:], in_=grouped[t][:])
            codes[t] = (words, plane)

        def multiply(t):
            words, plane = codes[t]
            sums[t] = []
            for half in range(N_OUT // BANK):
                acc = psum_mm.tile([P, BANK], F32, name="acc%d" % half)
                for g in range(PASSES):
                    nc.tensor.matmul_mx(
                        out=acc[:],
                        lhsT=words[:, g * P : (g + 1) * P].bitcast(FP8X4),
                        lhsT_scale=plane[:, g * P : (g + 1) * P],
                        rhs=w_words[:, g, 2 * BANK * half : 2 * BANK * (half + 1)].bitcast(FP4X4),
                        rhs_scale=w_scales[:, g, BANK * half : BANK * (half + 1)],
                        start=(g == 0),
                        stop=(g == PASSES - 1),
                    )
                sums[t].append(acc)

        def add_bias(t, half):
            if half == 0:
                li[t] = logits.tile([P, N_OUT], F32, name="li")
            cols = slice(BANK * half, BANK * (half + 1))
            nc.vector.tensor_tensor(out=li[t][:, cols], in0=sums[t][half][:], in1=bias[:, cols], op=ALU.add)

        def row_max(t):
            nc.vector.tensor_reduce(
                out=neg_max[:, col(t)], in_=li[t][:], axis=mybir.AxisListType.X, op=ALU.max, negate=True
            )

        def exponentials(t):
            unread = work.tile([P, N_OUT], BF16, name="unread_exp")
            nc.scalar.activation(
                out=unread[:], in_=li[t][:], func=ACT.Exp, bias=neg_max[:, col(t)], accum_out=exp_sum[:, col(t)]
            )

        def subtract(t, who):
            if who == "scalar":
                nc.scalar.activation(out=li[t][:], in_=li[t][:], func=ACT.Identity, bias=shift[:, col(t)], scale=1.0)
                nc.scalar.dma_start(out=out_rows[:, t, :], in_=li[t][:])
            else:
                engine = nc.vector if who == "vector" else nc.gpsimd
                engine.tensor_scalar(
                    out=li[t][:], in0=li[t][:], scalar1=1.0, scalar2=shift[:, col(t)], op0=ALU.mult, op1=ALU.add
                )
                nc.sync.dma_start(out=out_rows[:, t, :], in_=li[t][:])

        def log_guess(cols):
            nc.vector.tensor_scalar(
                out=log_guessed[:, cols], in0=exp_sum[:, cols].bitcast(I32),
                scalar1=GUESS_SCALE, scalar2=GUESS_OFFSET + AHEAD_AT_FIRST, op0=ALU.mult, op1=ALU.add,
            )

        def log_exp_first(cols):
            nc.scalar.activation(
                out=exp_neg_log[:, cols], in_=log_guessed[:, cols], func=ACT.Exp, scale=-1.0, bias=AHEAD_AT_FIRST
            )

        def log_exp_second(cols):
            nc.scalar.activation(
                out=exp_neg_log[:, cols], in_=log_better[:, cols], func=ACT.Exp, scale=-1.0, bias=AHEAD_AT_SECOND
            )

        def log_ratio(cols):
            nc.vector.tensor_tensor(out=ratio[:, cols], in0=exp_neg_log[:, cols], in1=exp_sum[:, cols], op=ALU.mult)

        def log_square(cols):
            nc.scalar.activation(out=square[:, cols], in_=ratio[:, cols], func=ACT.Square, scale=0.5, bias=-1.0)

        def log_first_step(cols):
            nc.vector.scalar_tensor_tensor(
                out=log_better[:, cols], in0=square[:, cols], scalar=-2.0, in1=log_guessed[:, cols],
                op0=ALU.mult, op1=ALU.add,
            )

        def log_rest(cols):
            nc.vector.tensor_tensor(out=rest[:, cols], in0=neg_max[:, cols], in1=log_better[:, cols], op=ALU.subtract)

        def log_shift(cols):
            nc.vector.scalar_tensor_tensor(
                out=shift[:, cols], in0=square[:, cols], scalar=2.0, in1=rest[:, cols], op0=ALU.mult, op1=ALU.add
            )

        upstream = []
        first = 0
        for size in NORM_GROUPS:
            upstream.extend([(relu_sum, t) for t in range(first, first + size)])
            upstream.extend([(squares, t) for t in range(first, first + size)])
            norm_after[first + size - 1] = slice(first, first + size)
            first += size
        assert first == TILES

        def run(stage, t, *more):
            if 0 <= t < TILES:
                stage(t, *more)

        VECTOR_PIECES = (
            (0, 2, log_guess),
            (1, 0, log_ratio), (1, 3, log_first_step), (1, 4, log_rest),
            (2, 0, log_ratio), (2, 3, log_shift),
        )
        SCALAR_PIECES = ((0, log_exp_first), (1, log_exp_second))
        SCALAR_SQUARES = (1, 2)
        in_gap = {}
        at_end = {}
        in_middle = {}
        ready = {}
        first = 0
        for size in GROUP_SIZES:
            cols = slice(first, first + size)
            start = first + size - 1 + LAG_EXP
            for later, gap, piece in VECTOR_PIECES:
                in_gap.setdefault((start + later, gap), []).append((piece, cols))
            for later, piece in SCALAR_PIECES:
                at_end.setdefault(start + later, []).append((piece, cols))
            for later in SCALAR_SQUARES:
                in_middle.setdefault(start + later, []).append((log_square, cols))
            begin = max(start + LOG_TURNS, min(start + LOG_TURNS + 1, (2 * TILES - LEAD) // 2))
            ready.setdefault(begin, []).extend(range(first, first + size))
            first += size
        assert first == TILES

        def pieces(found):
            for piece, cols in found:
                piece(cols)

        LAST_SQUARES_TURN = (2 * TILES - LEAD) // 2 - 1
        LAST_MAX_TURN = TILES - 1 + LAG_MAX
        for stage, t in upstream[:LEAD]:
            stage(t)
        waiting = []
        for turn in range(TILES + LAG_EXP + LOG_TURNS + 1):
            run(exponentials, turn - LAG_EXP)
            run(copy_out, turn - LAG_QUANTISE)
            run(add_bias, turn - LAG_BIAS_MAX, 0)
            pieces(in_gap.get((turn, 0), []))
            pieces(in_middle.get(turn, []))
            run(row_max, turn - LAG_MAX)
            pieces(in_gap.get((turn, 1), []))
            run(add_bias, turn - LAG_BIAS_MAX, 1)
            pieces(in_gap.get((turn, 2), []))
            run(multiply, turn - LAG_MULTIPLY)
            run(transpose, turn - LAG_TRANSPOSE)
            run(normalise, turn - LAG_NORMALISE)
            pieces(in_gap.get((turn, 3), []))
            waiting.extend(ready.get(turn, []))
            if turn > LAST_MAX_TURN:
                takers = ("vector", "vector")
            elif LAST_SQUARES_TURN < turn < LAST_MAX_TURN:
                takers = ("gpsimd", "scalar")
            else:
                takers = ("gpsimd",)
            for who in takers:
                if waiting and not (who == "scalar" and waiting[0] in ready.get(turn, [])):
                    subtract(waiting.pop(0), who)
            run(quantise, turn - LAG_QUANTISE)
            pieces(in_gap.get((turn, 4), []))
            for stage, t in upstream[LEAD + 2 * turn : LEAD + 2 * turn + 2]:
                stage(t)
            pieces(at_end.get(turn, []))
        assert not waiting
